import numpy as np
import ml_dtypes


def mxq(x, axis, fmt="e4m3"):
    dtype, down = {"e4m3": (ml_dtypes.float8_e4m3fn, 7), "e5m2": (ml_dtypes.float8_e5m2, 14)}[fmt]
    v = np.moveaxis(np.asarray(x, np.float32).astype(ml_dtypes.bfloat16).astype(np.float64), axis, -1)
    blocks = v.reshape(v.shape[:-1] + (-1, 32))
    amax = np.abs(blocks).max(-1, keepdims=True)
    byte = np.maximum(np.where(amax > 0, np.frexp(amax)[1] - 1 + 127, 0) - down, 1)
    scale = np.exp2(byte - 127.0)
    codes = (blocks / scale).astype(np.float32).astype(dtype).astype(np.float64)
    return np.moveaxis((codes * scale).reshape(v.shape), -1, axis)


WIDE = False


def mx_kscale(k):
    if not WIDE:
        return np.ones(k)
    levels = np.array([10, -10, 5, -5, 0])
    a = np.random.permutation(np.resize(levels, k // 512 * 4)).reshape(k // 512, 4)
    idx = np.arange(k)
    return np.exp2(a[idx // 512, idx % 128 // 32])


BF16 = ml_dtypes.bfloat16


def bf(x):
    return np.asarray(x, np.float32).astype(BF16)


def f64(x):
    return np.asarray(x).astype(np.float64)


N, E, D = 512, 16384, 128


def setup_inputs():
    s = mx_kscale(N)
    s = s / np.exp2(np.round(np.log2(s.mean())))
    return {"X": bf(np.random.standard_normal((N, D)) * 0.5 * np.sqrt(N) / s[:, None]),
            "H": bf(np.random.uniform(0.0, 1.0, (N, E)) * (16.0 / N) * s[:, None])}


def reference(X, H):
    Hf = f64(H)
    msg = mxq(Hf, 0, "e4m3").T @ mxq(f64(X), 0, "e4m3")
    with np.errstate(divide="ignore"):
        inv_deg = 1.0 / Hf.sum(axis=0)
    inv_deg = np.where(np.isinf(inv_deg), 0.0, inv_deg)
    return msg * inv_deg[:, None]

@@ -1,0 +1,232 @@
+from contextlib import ExitStack
+
+import concourse.mybir as mybir
+from concourse.masks import make_identity
+
+FLOPS = 2 * 512 * 16384 * 128
+
+FP8X4 = mybir.dt.float8_e4m3fn_x4
+BF16 = mybir.dt.bfloat16
+F32 = mybir.dt.float32
+U32 = mybir.dt.uint32
+U8 = mybir.dt.uint8
+ALU = mybir.AluOpType
+ACT = mybir.ActivationFunctionType
+
+P = 128
+PACK = 4
+UNIT = 512
+TH = 1
+T = 4 * TH
+G = P // T
+GROUP = P * T
+CHUNKS = [512, 512, 1024, 2048, 2048, 2048, 2048, 2048, 2048, 2048]
+STORE_GROUPS = 2
+PIN = True
+QV = 88
+EV_LAG = 3
+MX_BANKS = 5
+D2_COL = 256
+
+
+def tile_v2emsgpass_t_kernel(tc, X, H, out):
+    nc = tc.nc
+    n_edges = H.shape[1]
+    assert X.shape[0] == P * PACK and X.shape[1] == P and sum(CHUNKS) == n_edges
+
+    with ExitStack() as ctx:
+        if PIN:
+            ctx.enter_context(tc.manual_schedule())
+        const = ctx.enter_context(tc.tile_pool(name="const", bufs=1))
+        rawp = ctx.enter_context(tc.tile_pool(name="rawp", bufs=1))
+        outp = ctx.enter_context(tc.tile_pool(name="outp", bufs=1))
+        grp = ctx.enter_context(tc.tile_pool(name="grp", bufs=4))
+        cod = ctx.enter_context(tc.tile_pool(name="cod", bufs=4))
+        small = ctx.enter_context(tc.tile_pool(name="small", bufs=3))
+        ps_mx = ctx.enter_context(tc.psum_pool(name="ps_mx", bufs=MX_BANKS))
+        ps_dd = ctx.enter_context(tc.psum_pool(name="ps_dd", bufs=8 - MX_BANKS))
+
+        xraw = const.tile([P, PACK, P], BF16)
+        nc.sync.dma_start(out=xraw[:], in_=X.rearrange("(p j) d -> p j d", j=PACK))
+        raws = []
+        units = []
+        first_unit = []
+        c0 = 0
+        for b, w in enumerate(CHUNKS):
+            r = rawp.tile([P, PACK, w], BF16, name="raw%d" % b)
+            nc.sync.dma_start(
+                out=r[:], in_=H[:, c0:c0 + w].rearrange("(p j) w -> p j w", j=PACK)
+            )
+            raws.append(r)
+            first_unit.append(len(units))
+            for g in range(w // GROUP):
+                for th in range(TH):
+                    units.append((b, g, th, (c0 + g * GROUP) // GROUP))
+            c0 += w
+        n_units = len(units)
+        n_chunks = len(CHUNKS)
+
+        ident = const.tile([P, P], F32)
+        make_identity(nc, ident[:])
+        ones = const.tile([P, 2], BF16)
+        nc.vector.memset(ones[:], 1.0)
+        warm = const.tile([P, 2], F32)
+        nc.vector.memset(warm[:], 0.0)
+        warm2 = const.tile([P, 2], F32)
+        nc.scalar.activation(out=warm2[:], in_=warm[:], func=ACT.Copy)
+        sel = const.tile([P, T, P], F32)
+        nc.vector.memset(sel[:], 0.0)
+        lane = const.tile([P, T], F32)
+        nc.vector.tensor_reduce(
+            out=lane[:], in_=ident[:].rearrange("p (g t) -> p t g", t=T),
+            axis=mybir.AxisListType.X, op=ALU.add,
+        )
+        blk = const.tile([P, G], F32)
+        nc.vector.tensor_reduce(
+            out=blk[:], in_=ident[:].rearrange("p (g t) -> p g t", t=T),
+            axis=mybir.AxisListType.X, op=ALU.add,
+        )
+        for c in range(T):
+            nc.vector.tensor_copy(out=sel[:, c, c * G:(c + 1) * G], in_=blk[:])
+
+        xg = const.tile([P, P, PACK], BF16, align_bytes=64)
+        nc.vector.tensor_copy(out=xg[:], in_=xraw[:].rearrange("p j d -> p d j"))
+        xcodes = const.tile([P, P], U32, align_bytes=64)
+        xscales = const.tile([P, P], U8, align_bytes=64)
+
+        dds = {}
+        dexps = {}
+        degs = {}
+        invs = {}
+        grouped = {}
+        quantised = {}
+        banks = {}
+        otiles = {}
+
+        def degree_sums(b):
+            nt = CHUNKS[b] // P
+            dd = ps_dd.tile([P, 512], F32, tag="dd")
+            for c in range(nt):
+                for j in range(PACK):
+                    nc.tensor.matmul(
+                        out=dd[:, c:c + 1], lhsT=raws[b][:, j, c * P:(c + 1) * P],
+                        rhs=ones[:, 0:1], start=(j == 0), stop=(j == PACK - 1),
+                    )
+            dds[b] = dd
+
+        def degree_spread(b):
+            nt = CHUNKS[b] // P
+            ng = CHUNKS[b] // GROUP
+            dexp = small.tile([P, T, ng * T], F32, tag="dexp")
+            nc.vector.tensor_tensor(
+                out=dexp[:].rearrange("p c (g t) -> p c g t", t=T),
+                in0=dds[b][:, 0:nt].rearrange("p (g c) -> p c g", c=T)
+                .unsqueeze(3).to_broadcast([P, T, ng, T]),
+                in1=lane[:].unsqueeze(1).unsqueeze(1).to_broadcast([P, T, ng, T]),
+                op=ALU.mult,
+            )
+            for c in range(T):
+                nc.tensor.matmul(
+                    out=dds[b][:, D2_COL:D2_COL + ng * T], lhsT=sel[:, c, :], rhs=dexp[:, c, :],
+                    start=(c == 0), stop=(c == T - 1),
+                )
+
+        def degree_copy(b):
+            ng = CHUNKS[b] // GROUP
+            deg = small.tile([P, ng * T], F32, tag="deg")
+            nc.scalar.copy(out=deg[:], in_=dds[b][:, D2_COL:D2_COL + ng * T])
+            degs[b] = deg
+
+        def degree_invert(b):
+            ng = CHUNKS[b] // GROUP
+            deg = degs[b]
+            safe = small.tile([P, ng * T], F32, tag="safe")
+            nc.vector.scalar_tensor_tensor(
+                out=safe[:], in0=deg[:], scalar=0.0, in1=deg[:],
+                op0=ALU.is_equal, op1=ALU.add,
+            )
+            rec = small.tile([P, ng * T], F32, tag="rec")
+            nc.vector.reciprocal(out=rec[:], in_=safe[:])
+            inv = const.tile([P, ng * T], F32, name="inv%d" % b)
+            nc.vector.scalar_tensor_tensor(
+                out=inv[:], in0=deg[:], scalar=0.0, in1=rec[:],
+                op0=ALU.not_equal, op1=ALU.mult,
+            )
+            invs[b] = inv
+
+        def regroup(u):
+            b, g, th, gg = units[u]
+            gt = grp.tile([P, PACK * UNIT], BF16, align_bytes=64, tag="grouped")
+            block = raws[b][:, :, g * GROUP:(g + 1) * GROUP]
+            src = block.rearrange("p j (q h i) -> p h q j i", h=TH, i=4)[:, th]
+            dst = gt[:].rearrange("p (i q j) -> p q j i", i=4, j=PACK)
+            nc.vector.tensor_copy(out=dst[:, 0:QV], in_=src[:, 0:QV])
+            nc.scalar.copy(out=dst[:, QV:P], in_=src[:, QV:P])
+            grouped[u] = gt
+
+        def quantise(u):
+            codes = cod.tile([P, UNIT], U32, align_bytes=64, tag="codes")
+            scales = cod.tile([P, UNIT], U8, align_bytes=64, tag="scales")
+            nc.vector.quantize_mx(
+                out=codes[:].bitcast(FP8X4), scales=scales[:], in_=grouped[u][:]
+            )
+            quantised[u] = (codes, scales)
+
+        def multiply(u):
+            codes, scales = quantised[u]
+            acc = ps_mx.tile([P, 512], F32, tag="acc")
+            for i in range(4):
+                cols = slice(i * P, (i + 1) * P)
+                nc.tensor.matmul_mx(
+                    out=acc[:, cols],
+                    lhsT=codes[:, cols].bitcast(FP8X4), lhsT_scale=scales[:, cols],
+                    rhs=xcodes[:].bitcast(FP8X4), rhs_scale=xscales[:],
+                    start=True, stop=True,
+                )
+            banks[u] = acc
+
+        def evacuate(u):
+            b, g, th, gg = units[u]
+            s = gg // STORE_GROUPS
+            if s not in otiles:
+                otiles[s] = outp.tile([P, STORE_GROUPS * T * P], F32, name="o%d" % s)
+            o = otiles[s]
+            base = ((gg % STORE_GROUPS) * T + th * 4) * P
+            for i in range(4):
+                k = g * T + th * 4 + i
+                nc.scalar.activation(
+                    out=o[:, base + i * P:base + (i + 1) * P],
+                    in_=banks[u][:, i * P:(i + 1) * P],
+                    func=ACT.Copy, scale=invs[b][:, k:k + 1],
+                )
+            if gg % STORE_GROUPS == STORE_GROUPS - 1 and th == TH - 1:
+                e0 = s * STORE_GROUPS * GROUP
+                nc.sync.dma_start(
+                    out=out[e0:e0 + STORE_GROUPS * GROUP, :]
+                    .rearrange("(s q t) d -> q s (t d)", q=P, t=T),
+                    in_=o[:].rearrange("q (s x) -> q s x", s=STORE_GROUPS),
+                )
+
+        for step in range(-2, n_units + EV_LAG):
+            for b in range(n_chunks):
+                if first_unit[b] + 2 == step:
+                    degree_copy(b)
+            if 0 <= step + 1 < n_units:
+                regroup(step + 1)
+            if step == -1:
+                nc.vector.quantize_mx(
+                    out=xcodes[:].bitcast(FP8X4), scales=xscales[:],
+                    in_=xg[:].rearrange("p d j -> p (d j)"),
+                )
+            if 0 <= step < n_units:
+                quantise(step)
+                multiply(step)
+            for b in range(n_chunks):
+                if first_unit[b] == step:
+                    degree_spread(b)
+                if first_unit[b] + 2 == step:
+                    degree_invert(b)
+                if first_unit[b] - 2 == step:
+                    degree_sums(b)
+            if 0 <= step - EV_LAG < n_units:
+                evacuate(step - EV_LAG)

@@ -25,7 +25,8 @@ STORE_GROUPS = 2
 PIN = True
 QV = 88
 EV_LAG = 3
-MX_BANKS = 5
+MX_BANKS = 4
+DD_BANKS = 3
 D2_COL = 256
 
 
@@ -44,7 +45,8 @@ def tile_v2emsgpass_t_kernel(tc, X, H, out):
         cod = ctx.enter_context(tc.tile_pool(name="cod", bufs=4))
         small = ctx.enter_context(tc.tile_pool(name="small", bufs=3))
         ps_mx = ctx.enter_context(tc.psum_pool(name="ps_mx", bufs=MX_BANKS))
-        ps_dd = ctx.enter_context(tc.psum_pool(name="ps_dd", bufs=8 - MX_BANKS))
+        ps_dd = ctx.enter_context(tc.psum_pool(name="ps_dd", bufs=DD_BANKS))
+        ps_junk = ctx.enter_context(tc.psum_pool(name="ps_junk", bufs=1))
 
         xraw = const.tile([P, PACK, P], BF16)
         nc.sync.dma_start(out=xraw[:], in_=X.rearrange("(p j) d -> p j d", j=PACK))
@@ -94,8 +96,8 @@ def tile_v2emsgpass_t_kernel(tc, X, H, out):
         xcodes = const.tile([P, P], U32, align_bytes=64)
         xscales = const.tile([P, P], U8, align_bytes=64)
 
+        junk = ps_junk.tile([P, 512], F32)
         dds = {}
-        dexps = {}
         degs = {}
         invs = {}
         grouped = {}
@@ -184,6 +186,12 @@ def tile_v2emsgpass_t_kernel(tc, X, H, out):
                     start=True, stop=True,
                 )
             banks[u] = acc
+            nc.tensor.matmul_mx(
+                out=junk[:],
+                lhsT=xcodes[:].bitcast(FP8X4), lhsT_scale=xscales[:],
+                rhs=codes[:].bitcast(FP8X4), rhs_scale=scales[:],
+                start=True, stop=True,
+            )
 
         def evacuate(u):
             b, g, th, gg = units[u]

@@ -16,18 +16,18 @@ ACT = mybir.ActivationFunctionType
 P = 128
 PACK = 4
 UNIT = 512
-TH = 1
-T = 4 * TH
+T = 4
 G = P // T
 GROUP = P * T
 CHUNKS = [512, 512, 1024, 2048, 2048, 2048, 2048, 2048, 2048, 2048]
 STORE_GROUPS = 2
-PIN = True
 QV = 88
 EV_LAG = 3
 MX_BANKS = 4
 DD_BANKS = 3
 D2_COL = 256
+ONES = 11
+ONES_PITCH = 12
 
 
 def tile_v2emsgpass_t_kernel(tc, X, H, out):
@@ -36,8 +36,7 @@ def tile_v2emsgpass_t_kernel(tc, X, H, out):
     assert X.shape[0] == P * PACK and X.shape[1] == P and sum(CHUNKS) == n_edges
 
     with ExitStack() as ctx:
-        if PIN:
-            ctx.enter_context(tc.manual_schedule())
+        ctx.enter_context(tc.manual_schedule())
         const = ctx.enter_context(tc.tile_pool(name="const", bufs=1))
         rawp = ctx.enter_context(tc.tile_pool(name="rawp", bufs=1))
         outp = ctx.enter_context(tc.tile_pool(name="outp", bufs=1))
@@ -62,22 +61,19 @@ def tile_v2emsgpass_t_kernel(tc, X, H, out):
             raws.append(r)
             first_unit.append(len(units))
             for g in range(w // GROUP):
-                for th in range(TH):
-                    units.append((b, g, th, (c0 + g * GROUP) // GROUP))
+                units.append((b, g, (c0 + g * GROUP) // GROUP))
             c0 += w
         n_units = len(units)
         n_chunks = len(CHUNKS)
 
         ident = const.tile([P, P], F32)
         make_identity(nc, ident[:])
-        ones = const.tile([P, 2], BF16)
+        ones = const.tile([P, ONES_PITCH], BF16)
         nc.vector.memset(ones[:], 1.0)
         warm = const.tile([P, 2], F32)
         nc.vector.memset(warm[:], 0.0)
         warm2 = const.tile([P, 2], F32)
         nc.scalar.activation(out=warm2[:], in_=warm[:], func=ACT.Copy)
-        sel = const.tile([P, T, P], F32)
-        nc.vector.memset(sel[:], 0.0)
         lane = const.tile([P, T], F32)
         nc.vector.tensor_reduce(
             out=lane[:], in_=ident[:].rearrange("p (g t) -> p t g", t=T),
@@ -88,8 +84,11 @@ def tile_v2emsgpass_t_kernel(tc, X, H, out):
             out=blk[:], in_=ident[:].rearrange("p (g t) -> p g t", t=T),
             axis=mybir.AxisListType.X, op=ALU.add,
         )
-        for c in range(T):
-            nc.vector.tensor_copy(out=sel[:, c, c * G:(c + 1) * G], in_=blk[:])
+        rep = const.tile([P, P], F32)
+        nc.vector.tensor_copy(
+            out=rep[:].rearrange("p (c g) -> p c g", c=T),
+            in_=blk[:].unsqueeze(1).to_broadcast([P, T, G]),
+        )
 
         xg = const.tile([P, P, PACK], BF16, align_bytes=64)
         nc.vector.tensor_copy(out=xg[:], in_=xraw[:].rearrange("p j d -> p d j"))
@@ -105,38 +104,44 @@ def tile_v2emsgpass_t_kernel(tc, X, H, out):
         banks = {}
         otiles = {}
 
-        def degree_sums(b):
+        def degree_sums(b, half):
             nt = CHUNKS[b] // P
-            dd = ps_dd.tile([P, 512], F32, tag="dd")
-            for c in range(nt):
+            if half == 0:
+                dds[b] = ps_dd.tile([P, 512], F32, tag="dd", name="dd")
+            dd = dds[b]
+            for c in range(half * nt // 2, (half + 1) * nt // 2):
                 for j in range(PACK):
                     nc.tensor.matmul(
-                        out=dd[:, c:c + 1], lhsT=raws[b][:, j, c * P:(c + 1) * P],
-                        rhs=ones[:, 0:1], start=(j == 0), stop=(j == PACK - 1),
+                        out=dd[:, c * ONES_PITCH:c * ONES_PITCH + ONES],
+                        lhsT=raws[b][:, j, c * P:(c + 1) * P],
+                        rhs=ones[:, 0:ONES], start=(j == 0), stop=(j == PACK - 1),
                     )
-            dds[b] = dd
 
         def degree_spread(b):
             nt = CHUNKS[b] // P
             ng = CHUNKS[b] // GROUP
             dexp = small.tile([P, T, ng * T], F32, tag="dexp")
+            d1 = dds[b][:, 0:nt * ONES_PITCH].rearrange(
+                "p (g c n) -> p c g n", c=T, n=ONES_PITCH
+            )[:, :, :, 0:1]
             nc.vector.tensor_tensor(
                 out=dexp[:].rearrange("p c (g t) -> p c g t", t=T),
-                in0=dds[b][:, 0:nt].rearrange("p (g c) -> p c g", c=T)
-                .unsqueeze(3).to_broadcast([P, T, ng, T]),
+                in0=d1.to_broadcast([P, T, ng, T]),
                 in1=lane[:].unsqueeze(1).unsqueeze(1).to_broadcast([P, T, ng, T]),
                 op=ALU.mult,
             )
-            for c in range(T):
-                nc.tensor.matmul(
-                    out=dds[b][:, D2_COL:D2_COL + ng * T], lhsT=sel[:, c, :], rhs=dexp[:, c, :],
-                    start=(c == 0), stop=(c == T - 1),
-                )
+            nc.tensor.matmul(
+                out=dds[b][:, D2_COL:D2_COL + T * ng * T], lhsT=rep[:],
+                rhs=dexp[:].rearrange("p c x -> p (c x)"), start=True, stop=True,
+            )
 
         def degree_copy(b):
             ng = CHUNKS[b] // GROUP
             deg = small.tile([P, ng * T], F32, tag="deg")
-            nc.scalar.copy(out=deg[:], in_=dds[b][:, D2_COL:D2_COL + ng * T])
+            for c in range(T):
+                rows = slice(c * G, (c + 1) * G)
+                col = D2_COL + c * ng * T
+                nc.scalar.copy(out=deg[rows, :], in_=dds[b][rows, col:col + ng * T])
             degs[b] = deg
 
         def degree_invert(b):
@@ -157,10 +162,10 @@ def tile_v2emsgpass_t_kernel(tc, X, H, out):
             invs[b] = inv
 
         def regroup(u):
-            b, g, th, gg = units[u]
+            b, g, gg = units[u]
             gt = grp.tile([P, PACK * UNIT], BF16, align_bytes=64, tag="grouped")
             block = raws[b][:, :, g * GROUP:(g + 1) * GROUP]
-            src = block.rearrange("p j (q h i) -> p h q j i", h=TH, i=4)[:, th]
+            src = block.rearrange("p j (q i) -> p q j i", i=4)
             dst = gt[:].rearrange("p (i q j) -> p q j i", i=4, j=PACK)
             nc.vector.tensor_copy(out=dst[:, 0:QV], in_=src[:, 0:QV])
             nc.scalar.copy(out=dst[:, QV:P], in_=src[:, QV:P])
@@ -186,6 +191,9 @@ def tile_v2emsgpass_t_kernel(tc, X, H, out):
                     start=True, stop=True,
                 )
             banks[u] = acc
+
+        def keep_clock(u):
+            codes, scales = quantised[u]
             nc.tensor.matmul_mx(
                 out=junk[:],
                 lhsT=xcodes[:].bitcast(FP8X4), lhsT_scale=xscales[:],
@@ -194,20 +202,20 @@ def tile_v2emsgpass_t_kernel(tc, X, H, out):
             )
 
         def evacuate(u):
-            b, g, th, gg = units[u]
+            b, g, gg = units[u]
             s = gg // STORE_GROUPS
             if s not in otiles:
                 otiles[s] = outp.tile([P, STORE_GROUPS * T * P], F32, name="o%d" % s)
             o = otiles[s]
-            base = ((gg % STORE_GROUPS) * T + th * 4) * P
+            base = (gg % STORE_GROUPS) * T * P
             for i in range(4):
-                k = g * T + th * 4 + i
+                k = g * T + i
                 nc.scalar.activation(
                     out=o[:, base + i * P:base + (i + 1) * P],
                     in_=banks[u][:, i * P:(i + 1) * P],
                     func=ACT.Copy, scale=invs[b][:, k:k + 1],
                 )
-            if gg % STORE_GROUPS == STORE_GROUPS - 1 and th == TH - 1:
+            if gg % STORE_GROUPS == STORE_GROUPS - 1:
                 e0 = s * STORE_GROUPS * GROUP
                 nc.sync.dma_start(
                     out=out[e0:e0 + STORE_GROUPS * GROUP, :]
@@ -232,9 +240,14 @@ def tile_v2emsgpass_t_kernel(tc, X, H, out):
             for b in range(n_chunks):
                 if first_unit[b] == step:
                     degree_spread(b)
+            if 0 <= step < n_units:
+                keep_clock(step)
+            for b in range(n_chunks):
                 if first_unit[b] + 2 == step:
                     degree_invert(b)
+                if first_unit[b] - 1 == step:
+                    degree_sums(b, 1)
                 if first_unit[b] - 2 == step:
-                    degree_sums(b)
+                    degree_sums(b, 0)
             if 0 <= step - EV_LAG < n_units:
                 evacuate(step - EV_LAG)

@@ -16,18 +16,18 @@ ACT = mybir.ActivationFunctionType
 P = 128
 PACK = 4
 UNIT = 512
-T = 4
+TH = 1
+T = 4 * TH
 G = P // T
 GROUP = P * T
 CHUNKS = [512, 512, 1024, 2048, 2048, 2048, 2048, 2048, 2048, 2048]
 STORE_GROUPS = 2
-QV = 88
+PIN = True
+QV = 104
 EV_LAG = 3
 MX_BANKS = 4
 DD_BANKS = 3
 D2_COL = 256
-ONES = 11
-ONES_PITCH = 12
 
 
 def tile_v2emsgpass_t_kernel(tc, X, H, out):
@@ -36,7 +36,8 @@ def tile_v2emsgpass_t_kernel(tc, X, H, out):
     assert X.shape[0] == P * PACK and X.shape[1] == P and sum(CHUNKS) == n_edges
 
     with ExitStack() as ctx:
-        ctx.enter_context(tc.manual_schedule())
+        if PIN:
+            ctx.enter_context(tc.manual_schedule())
         const = ctx.enter_context(tc.tile_pool(name="const", bufs=1))
         rawp = ctx.enter_context(tc.tile_pool(name="rawp", bufs=1))
         outp = ctx.enter_context(tc.tile_pool(name="outp", bufs=1))
@@ -61,19 +62,22 @@ def tile_v2emsgpass_t_kernel(tc, X, H, out):
             raws.append(r)
             first_unit.append(len(units))
             for g in range(w // GROUP):
-                units.append((b, g, (c0 + g * GROUP) // GROUP))
+                for th in range(TH):
+                    units.append((b, g, th, (c0 + g * GROUP) // GROUP))
             c0 += w
         n_units = len(units)
         n_chunks = len(CHUNKS)
 
         ident = const.tile([P, P], F32)
         make_identity(nc, ident[:])
-        ones = const.tile([P, ONES_PITCH], BF16)
+        ones = const.tile([P, 2], BF16)
         nc.vector.memset(ones[:], 1.0)
         warm = const.tile([P, 2], F32)
         nc.vector.memset(warm[:], 0.0)
         warm2 = const.tile([P, 2], F32)
         nc.scalar.activation(out=warm2[:], in_=warm[:], func=ACT.Copy)
+        sel = const.tile([P, T, P], F32)
+        nc.vector.memset(sel[:], 0.0)
         lane = const.tile([P, T], F32)
         nc.vector.tensor_reduce(
             out=lane[:], in_=ident[:].rearrange("p (g t) -> p t g", t=T),
@@ -84,11 +88,8 @@ def tile_v2emsgpass_t_kernel(tc, X, H, out):
             out=blk[:], in_=ident[:].rearrange("p (g t) -> p g t", t=T),
             axis=mybir.AxisListType.X, op=ALU.add,
         )
-        rep = const.tile([P, P], F32)
-        nc.vector.tensor_copy(
-            out=rep[:].rearrange("p (c g) -> p c g", c=T),
-            in_=blk[:].unsqueeze(1).to_broadcast([P, T, G]),
-        )
+        for c in range(T):
+            nc.vector.tensor_copy(out=sel[:, c, c * G:(c + 1) * G], in_=blk[:])
 
         xg = const.tile([P, P, PACK], BF16, align_bytes=64)
         nc.vector.tensor_copy(out=xg[:], in_=xraw[:].rearrange("p j d -> p d j"))
@@ -104,44 +105,38 @@ def tile_v2emsgpass_t_kernel(tc, X, H, out):
         banks = {}
         otiles = {}
 
-        def degree_sums(b, half):
+        def degree_sums(b):
             nt = CHUNKS[b] // P
-            if half == 0:
-                dds[b] = ps_dd.tile([P, 512], F32, tag="dd", name="dd")
-            dd = dds[b]
-            for c in range(half * nt // 2, (half + 1) * nt // 2):
+            dd = ps_dd.tile([P, 512], F32, tag="dd")
+            for c in range(nt):
                 for j in range(PACK):
                     nc.tensor.matmul(
-                        out=dd[:, c * ONES_PITCH:c * ONES_PITCH + ONES],
-                        lhsT=raws[b][:, j, c * P:(c + 1) * P],
-                        rhs=ones[:, 0:ONES], start=(j == 0), stop=(j == PACK - 1),
+                        out=dd[:, c:c + 1], lhsT=raws[b][:, j, c * P:(c + 1) * P],
+                        rhs=ones[:, 0:1], start=(j == 0), stop=(j == PACK - 1),
                     )
+            dds[b] = dd
 
         def degree_spread(b):
             nt = CHUNKS[b] // P
             ng = CHUNKS[b] // GROUP
             dexp = small.tile([P, T, ng * T], F32, tag="dexp")
-            d1 = dds[b][:, 0:nt * ONES_PITCH].rearrange(
-                "p (g c n) -> p c g n", c=T, n=ONES_PITCH
-            )[:, :, :, 0:1]
             nc.vector.tensor_tensor(
                 out=dexp[:].rearrange("p c (g t) -> p c g t", t=T),
-                in0=d1.to_broadcast([P, T, ng, T]),
+                in0=dds[b][:, 0:nt].rearrange("p (g c) -> p c g", c=T)
+                .unsqueeze(3).to_broadcast([P, T, ng, T]),
                 in1=lane[:].unsqueeze(1).unsqueeze(1).to_broadcast([P, T, ng, T]),
                 op=ALU.mult,
             )
-            nc.tensor.matmul(
-                out=dds[b][:, D2_COL:D2_COL + T * ng * T], lhsT=rep[:],
-                rhs=dexp[:].rearrange("p c x -> p (c x)"), start=True, stop=True,
-            )
+            for c in range(T):
+                nc.tensor.matmul(
+                    out=dds[b][:, D2_COL:D2_COL + ng * T], lhsT=sel[:, c, :], rhs=dexp[:, c, :],
+                    start=(c == 0), stop=(c == T - 1),
+                )
 
         def degree_copy(b):
             ng = CHUNKS[b] // GROUP
             deg = small.tile([P, ng * T], F32, tag="deg")
-            for c in range(T):
-                rows = slice(c * G, (c + 1) * G)
-                col = D2_COL + c * ng * T
-                nc.scalar.copy(out=deg[rows, :], in_=dds[b][rows, col:col + ng * T])
+            nc.scalar.copy(out=deg[:], in_=dds[b][:, D2_COL:D2_COL + ng * T])
             degs[b] = deg
 
         def degree_invert(b):
@@ -162,10 +157,10 @@ def tile_v2emsgpass_t_kernel(tc, X, H, out):
             invs[b] = inv
 
         def regroup(u):
-            b, g, gg = units[u]
+            b, g, th, gg = units[u]
             gt = grp.tile([P, PACK * UNIT], BF16, align_bytes=64, tag="grouped")
             block = raws[b][:, :, g * GROUP:(g + 1) * GROUP]
-            src = block.rearrange("p j (q i) -> p q j i", i=4)
+            src = block.rearrange("p j (q h i) -> p h q j i", h=TH, i=4)[:, th]
             dst = gt[:].rearrange("p (i q j) -> p q j i", i=4, j=PACK)
             nc.vector.tensor_copy(out=dst[:, 0:QV], in_=src[:, 0:QV])
             nc.scalar.copy(out=dst[:, QV:P], in_=src[:, QV:P])
@@ -191,9 +186,6 @@ def tile_v2emsgpass_t_kernel(tc, X, H, out):
                     start=True, stop=True,
                 )
             banks[u] = acc
-
-        def keep_clock(u):
-            codes, scales = quantised[u]
             nc.tensor.matmul_mx(
                 out=junk[:],
                 lhsT=xcodes[:].bitcast(FP8X4), lhsT_scale=xscales[:],
@@ -202,20 +194,20 @@ def tile_v2emsgpass_t_kernel(tc, X, H, out):
             )
 
         def evacuate(u):
-            b, g, gg = units[u]
+            b, g, th, gg = units[u]
             s = gg // STORE_GROUPS
             if s not in otiles:
                 otiles[s] = outp.tile([P, STORE_GROUPS * T * P], F32, name="o%d" % s)
             o = otiles[s]
-            base = (gg % STORE_GROUPS) * T * P
+            base = ((gg % STORE_GROUPS) * T + th * 4) * P
             for i in range(4):
-                k = g * T + i
+                k = g * T + th * 4 + i
                 nc.scalar.activation(
                     out=o[:, base + i * P:base + (i + 1) * P],
                     in_=banks[u][:, i * P:(i + 1) * P],
                     func=ACT.Copy, scale=invs[b][:, k:k + 1],
                 )
-            if gg % STORE_GROUPS == STORE_GROUPS - 1:
+            if gg % STORE_GROUPS == STORE_GROUPS - 1 and th == TH - 1:
                 e0 = s * STORE_GROUPS * GROUP
                 nc.sync.dma_start(
                     out=out[e0:e0 + STORE_GROUPS * GROUP, :]
@@ -240,14 +232,9 @@ def tile_v2emsgpass_t_kernel(tc, X, H, out):
             for b in range(n_chunks):
                 if first_unit[b] == step:
                     degree_spread(b)
-            if 0 <= step < n_units:
-                keep_clock(step)
-            for b in range(n_chunks):
                 if first_unit[b] + 2 == step:
                     degree_invert(b)
-                if first_unit[b] - 1 == step:
-                    degree_sums(b, 1)
                 if first_unit[b] - 2 == step:
-                    degree_sums(b, 0)
+                    degree_sums(b)
             if 0 <= step - EV_LAG < n_units:
                 evacuate(step - EV_LAG)

@@ -23,7 +23,7 @@ GROUP = P * T
 CHUNKS = [512, 512, 1024, 2048, 2048, 2048, 2048, 2048, 2048, 2048]
 STORE_GROUPS = 2
 PIN = True
-QV = 104
+QV = 72
 EV_LAG = 3
 MX_BANKS = 4
 DD_BANKS = 3
@@ -200,14 +200,27 @@ def tile_v2emsgpass_t_kernel(tc, X, H, out):
                 otiles[s] = outp.tile([P, STORE_GROUPS * T * P], F32, name="o%d" % s)
             o = otiles[s]
             base = ((gg % STORE_GROUPS) * T + th * 4) * P
-            for i in range(4):
-                k = g * T + th * 4 + i
-                nc.scalar.activation(
-                    out=o[:, base + i * P:base + (i + 1) * P],
-                    in_=banks[u][:, i * P:(i + 1) * P],
-                    func=ACT.Copy, scale=invs[b][:, k:k + 1],
+            if u >= n_units - 2:
+                nc.vector.tensor_tensor(
+                    out=o[:, base:base + UNIT].rearrange("p (t d) -> p t d", t=T),
+                    in0=banks[u][:].rearrange("p (t d) -> p t d", t=T),
+                    in1=invs[b][:, g * T:(g + 1) * T].unsqueeze(2).to_broadcast([P, T, P]),
+                    op=ALU.mult,
                 )
-            if gg % STORE_GROUPS == STORE_GROUPS - 1 and th == TH - 1:
+            else:
+                for i in range(4):
+                    k = g * T + th * 4 + i
+                    nc.scalar.activation(
+                        out=o[:, base + i * P:base + (i + 1) * P],
+                        in_=banks[u][:, i * P:(i + 1) * P],
+                        func=ACT.Copy, scale=invs[b][:, k:k + 1],
+                    )
+            if u >= n_units - 2:
+                nc.sync.dma_start(
+                    out=out[u * UNIT:(u + 1) * UNIT, :].rearrange("(q t) d -> q (t d)", t=T),
+                    in_=o[:, base:base + UNIT],
+                )
+            elif gg % STORE_GROUPS == STORE_GROUPS - 1 and th == TH - 1:
                 e0 = s * STORE_GROUPS * GROUP
                 nc.sync.dma_start(
                     out=out[e0:e0 + STORE_GROUPS * GROUP, :]

@@ -23,7 +23,7 @@ GROUP = P * T
 CHUNKS = [512, 512, 1024, 2048, 2048, 2048, 2048, 2048, 2048, 2048]
 STORE_GROUPS = 2
 PIN = True
-QV = 72
+QV = 80
 EV_LAG = 3
 MX_BANKS = 4
 DD_BANKS = 3
@@ -41,8 +41,8 @@ def tile_v2emsgpass_t_kernel(tc, X, H, out):
         const = ctx.enter_context(tc.tile_pool(name="const", bufs=1))
         rawp = ctx.enter_context(tc.tile_pool(name="rawp", bufs=1))
         outp = ctx.enter_context(tc.tile_pool(name="outp", bufs=1))
-        grp = ctx.enter_context(tc.tile_pool(name="grp", bufs=4))
-        cod = ctx.enter_context(tc.tile_pool(name="cod", bufs=4))
+        grp = ctx.enter_context(tc.tile_pool(name="grp", bufs=2))
+        cod = ctx.enter_context(tc.tile_pool(name="cod", bufs=3))
         small = ctx.enter_context(tc.tile_pool(name="small", bufs=3))
         ps_mx = ctx.enter_context(tc.psum_pool(name="ps_mx", bufs=MX_BANKS))
         ps_dd = ctx.enter_context(tc.psum_pool(name="ps_dd", bufs=DD_BANKS))
@@ -158,38 +158,43 @@ def tile_v2emsgpass_t_kernel(tc, X, H, out):
 
         def regroup(u):
             b, g, th, gg = units[u]
-            gt = grp.tile([P, PACK * UNIT], BF16, align_bytes=64, tag="grouped")
+            if u % 2 == 0:
+                grouped[u // 2] = grp.tile(
+                    [P, 2 * PACK * UNIT], BF16, align_bytes=64, tag="grouped", name="grouped"
+                )
+            half = (u % 2) * PACK * UNIT
+            gt = grouped[u // 2][:, half:half + PACK * UNIT]
             block = raws[b][:, :, g * GROUP:(g + 1) * GROUP]
             src = block.rearrange("p j (q h i) -> p h q j i", h=TH, i=4)[:, th]
-            dst = gt[:].rearrange("p (i q j) -> p q j i", i=4, j=PACK)
+            dst = gt.rearrange("p (i q j) -> p q j i", i=4, j=PACK)
             nc.vector.tensor_copy(out=dst[:, 0:QV], in_=src[:, 0:QV])
             nc.scalar.copy(out=dst[:, QV:P], in_=src[:, QV:P])
-            grouped[u] = gt
 
-        def quantise(u):
-            codes = cod.tile([P, UNIT], U32, align_bytes=64, tag="codes")
-            scales = cod.tile([P, UNIT], U8, align_bytes=64, tag="scales")
+        def quantise(pair):
+            codes = cod.tile([P, 2 * UNIT], U32, align_bytes=64, tag="codes")
+            scales = cod.tile([P, 2 * UNIT], U8, align_bytes=64, tag="scales")
             nc.vector.quantize_mx(
-                out=codes[:].bitcast(FP8X4), scales=scales[:], in_=grouped[u][:]
+                out=codes[:].bitcast(FP8X4), scales=scales[:], in_=grouped[pair][:]
             )
-            quantised[u] = (codes, scales)
+            quantised[pair] = (codes, scales)
 
         def multiply(u):
-            codes, scales = quantised[u]
+            codes, scales = quantised[u // 2]
             acc = ps_mx.tile([P, 512], F32, tag="acc")
             for i in range(4):
-                cols = slice(i * P, (i + 1) * P)
+                cols = slice((u % 2) * UNIT + i * P, (u % 2) * UNIT + (i + 1) * P)
                 nc.tensor.matmul_mx(
-                    out=acc[:, cols],
+                    out=acc[:, i * P:(i + 1) * P],
                     lhsT=codes[:, cols].bitcast(FP8X4), lhsT_scale=scales[:, cols],
                     rhs=xcodes[:].bitcast(FP8X4), rhs_scale=xscales[:],
                     start=True, stop=True,
                 )
             banks[u] = acc
+            cols = slice((u % 2) * UNIT, (u % 2 + 1) * UNIT)
             nc.tensor.matmul_mx(
                 out=junk[:],
                 lhsT=xcodes[:].bitcast(FP8X4), lhsT_scale=xscales[:],
-                rhs=codes[:].bitcast(FP8X4), rhs_scale=scales[:],
+                rhs=codes[:, cols].bitcast(FP8X4), rhs_scale=scales[:, cols],
                 start=True, stop=True,
             )
 
@@ -239,8 +244,9 @@ def tile_v2emsgpass_t_kernel(tc, X, H, out):
                     out=xcodes[:].bitcast(FP8X4), scales=xscales[:],
                     in_=xg[:].rearrange("p d j -> p (d j)"),
                 )
-            if 0 <= step < n_units:
-                quantise(step)
+            if 0 <= step < n_units and step % 2 == 1:
+                quantise(step // 2)
+                multiply(step - 1)
                 multiply(step)
             for b in range(n_chunks):
                 if first_unit[b] == step:

@@ -25,7 +25,9 @@ STORE_GROUPS = 2
 PIN = True
 QV = 80
 EV_LAG = 3
-MX_BANKS = 4
+MX_BANKS = 5
+ONES = 11
+PITCH = 12
 DD_BANKS = 3
 D2_COL = 256
 
@@ -40,13 +42,12 @@ def tile_v2emsgpass_t_kernel(tc, X, H, out):
             ctx.enter_context(tc.manual_schedule())
         const = ctx.enter_context(tc.tile_pool(name="const", bufs=1))
         rawp = ctx.enter_context(tc.tile_pool(name="rawp", bufs=1))
-        outp = ctx.enter_context(tc.tile_pool(name="outp", bufs=1))
-        grp = ctx.enter_context(tc.tile_pool(name="grp", bufs=2))
-        cod = ctx.enter_context(tc.tile_pool(name="cod", bufs=3))
+        outp = ctx.enter_context(tc.tile_pool(name="outp", bufs=12))
+        grp = ctx.enter_context(tc.tile_pool(name="grp", bufs=3))
+        cod = ctx.enter_context(tc.tile_pool(name="cod", bufs=4))
         small = ctx.enter_context(tc.tile_pool(name="small", bufs=3))
         ps_mx = ctx.enter_context(tc.psum_pool(name="ps_mx", bufs=MX_BANKS))
         ps_dd = ctx.enter_context(tc.psum_pool(name="ps_dd", bufs=DD_BANKS))
-        ps_junk = ctx.enter_context(tc.psum_pool(name="ps_junk", bufs=1))
 
         xraw = const.tile([P, PACK, P], BF16)
         nc.sync.dma_start(out=xraw[:], in_=X.rearrange("(p j) d -> p j d", j=PACK))
@@ -70,7 +71,7 @@ def tile_v2emsgpass_t_kernel(tc, X, H, out):
 
         ident = const.tile([P, P], F32)
         make_identity(nc, ident[:])
-        ones = const.tile([P, 2], BF16)
+        ones = const.tile([P, PITCH], BF16)
         nc.vector.memset(ones[:], 1.0)
         warm = const.tile([P, 2], F32)
         nc.vector.memset(warm[:], 0.0)
@@ -96,7 +97,6 @@ def tile_v2emsgpass_t_kernel(tc, X, H, out):
         xcodes = const.tile([P, P], U32, align_bytes=64)
         xscales = const.tile([P, P], U8, align_bytes=64)
 
-        junk = ps_junk.tile([P, 512], F32)
         dds = {}
         degs = {}
         invs = {}
@@ -111,8 +111,9 @@ def tile_v2emsgpass_t_kernel(tc, X, H, out):
             for c in range(nt):
                 for j in range(PACK):
                     nc.tensor.matmul(
-                        out=dd[:, c:c + 1], lhsT=raws[b][:, j, c * P:(c + 1) * P],
-                        rhs=ones[:, 0:1], start=(j == 0), stop=(j == PACK - 1),
+                        out=dd[:, c * PITCH:c * PITCH + ONES],
+                        lhsT=raws[b][:, j, c * P:(c + 1) * P],
+                        rhs=ones[:, 0:ONES], start=(j == 0), stop=(j == PACK - 1),
                     )
             dds[b] = dd
 
@@ -122,8 +123,8 @@ def tile_v2emsgpass_t_kernel(tc, X, H, out):
             dexp = small.tile([P, T, ng * T], F32, tag="dexp")
             nc.vector.tensor_tensor(
                 out=dexp[:].rearrange("p c (g t) -> p c g t", t=T),
-                in0=dds[b][:, 0:nt].rearrange("p (g c) -> p c g", c=T)
-                .unsqueeze(3).to_broadcast([P, T, ng, T]),
+                in0=dds[b][:, 0:nt * PITCH].rearrange("p (g c n) -> p c g n", c=T, n=PITCH)
+                [:, :, :, 0:1].to_broadcast([P, T, ng, T]),
                 in1=lane[:].unsqueeze(1).unsqueeze(1).to_broadcast([P, T, ng, T]),
                 op=ALU.mult,
             )
@@ -156,9 +157,9 @@ def tile_v2emsgpass_t_kernel(tc, X, H, out):
             )
             invs[b] = inv
 
-        def regroup(u):
+        def regroup(u, on_scalar):
             b, g, th, gg = units[u]
-            if u % 2 == 0:
+            if u % 2 == 0 and on_scalar:
                 grouped[u // 2] = grp.tile(
                     [P, 2 * PACK * UNIT], BF16, align_bytes=64, tag="grouped", name="grouped"
                 )
@@ -167,8 +168,10 @@ def tile_v2emsgpass_t_kernel(tc, X, H, out):
             block = raws[b][:, :, g * GROUP:(g + 1) * GROUP]
             src = block.rearrange("p j (q h i) -> p h q j i", h=TH, i=4)[:, th]
             dst = gt.rearrange("p (i q j) -> p q j i", i=4, j=PACK)
-            nc.vector.tensor_copy(out=dst[:, 0:QV], in_=src[:, 0:QV])
-            nc.scalar.copy(out=dst[:, QV:P], in_=src[:, QV:P])
+            if on_scalar:
+                nc.scalar.copy(out=dst[:, QV:P], in_=src[:, QV:P])
+            else:
+                nc.vector.tensor_copy(out=dst[:, 0:QV], in_=src[:, 0:QV])
 
         def quantise(pair):
             codes = cod.tile([P, 2 * UNIT], U32, align_bytes=64, tag="codes")
@@ -181,6 +184,14 @@ def tile_v2emsgpass_t_kernel(tc, X, H, out):
         def multiply(u):
             codes, scales = quantised[u // 2]
             acc = ps_mx.tile([P, 512], F32, tag="acc")
+            if u < n_units - 2:
+                cols = slice((u % 2) * UNIT, (u % 2 + 1) * UNIT)
+                nc.tensor.matmul_mx(
+                    out=acc[:],
+                    lhsT=xcodes[:].bitcast(FP8X4), lhsT_scale=xscales[:],
+                    rhs=codes[:, cols].bitcast(FP8X4), rhs_scale=scales[:, cols],
+                    start=True, stop=True,
+                )
             for i in range(4):
                 cols = slice((u % 2) * UNIT + i * P, (u % 2) * UNIT + (i + 1) * P)
                 nc.tensor.matmul_mx(
@@ -190,19 +201,12 @@ def tile_v2emsgpass_t_kernel(tc, X, H, out):
                     start=True, stop=True,
                 )
             banks[u] = acc
-            cols = slice((u % 2) * UNIT, (u % 2 + 1) * UNIT)
-            nc.tensor.matmul_mx(
-                out=junk[:],
-                lhsT=xcodes[:].bitcast(FP8X4), lhsT_scale=xscales[:],
-                rhs=codes[:, cols].bitcast(FP8X4), rhs_scale=scales[:, cols],
-                start=True, stop=True,
-            )
 
         def evacuate(u):
             b, g, th, gg = units[u]
             s = gg // STORE_GROUPS
             if s not in otiles:
-                otiles[s] = outp.tile([P, STORE_GROUPS * T * P], F32, name="o%d" % s)
+                otiles[s] = outp.tile([P, STORE_GROUPS * T * P], F32, tag="o", name="o%d" % s)
             o = otiles[s]
             base = ((gg % STORE_GROUPS) * T + th * 4) * P
             if u >= n_units - 2:
@@ -237,8 +241,10 @@ def tile_v2emsgpass_t_kernel(tc, X, H, out):
             for b in range(n_chunks):
                 if first_unit[b] + 2 == step:
                     degree_copy(b)
+            if 0 <= step + 2 < n_units:
+                regroup(step + 2, True)
             if 0 <= step + 1 < n_units:
-                regroup(step + 1)
+                regroup(step + 1, False)
             if step == -1:
                 nc.vector.quantize_mx(
                     out=xcodes[:].bitcast(FP8X4), scales=xscales[:],

@@ -20,7 +20,7 @@ TH = 1
 T = 4 * TH
 G = P // T
 GROUP = P * T
-CHUNKS = [512, 512, 1024, 2048, 2048, 2048, 2048, 2048, 2048, 2048]
+CHUNKS = [512, 512, 1024, 1024, 1024, 2048, 2048, 2048, 2048, 2048, 2048]
 STORE_GROUPS = 2
 PIN = True
 QV = 80

from contextlib import ExitStack

import concourse.mybir as mybir
from concourse.masks import make_identity

FLOPS = 2 * 512 * 16384 * 128

FP8X4 = mybir.dt.float8_e4m3fn_x4
BF16 = mybir.dt.bfloat16
F32 = mybir.dt.float32
U32 = mybir.dt.uint32
U8 = mybir.dt.uint8
ALU = mybir.AluOpType
ACT = mybir.ActivationFunctionType

P = 128
PACK = 4
UNIT = 512
TH = 1
T = 4 * TH
G = P // T
GROUP = P * T
CHUNKS = [512, 512, 1024, 1024, 1024, 2048, 2048, 2048, 2048, 2048, 2048]
STORE_GROUPS = 2
PIN = True
QV = 80
EV_LAG = 3
MX_BANKS = 5
ONES = 11
PITCH = 12
DD_BANKS = 3
D2_COL = 256


def tile_v2emsgpass_t_kernel(tc, X, H, out):
    nc = tc.nc
    n_edges = H.shape[1]
    assert X.shape[0] == P * PACK and X.shape[1] == P and sum(CHUNKS) == n_edges

    with ExitStack() as ctx:
        if PIN:
            ctx.enter_context(tc.manual_schedule())
        const = ctx.enter_context(tc.tile_pool(name="const", bufs=1))
        rawp = ctx.enter_context(tc.tile_pool(name="rawp", bufs=1))
        outp = ctx.enter_context(tc.tile_pool(name="outp", bufs=12))
        grp = ctx.enter_context(tc.tile_pool(name="grp", bufs=3))
        cod = ctx.enter_context(tc.tile_pool(name="cod", bufs=4))
        small = ctx.enter_context(tc.tile_pool(name="small", bufs=3))
        ps_mx = ctx.enter_context(tc.psum_pool(name="ps_mx", bufs=MX_BANKS))
        ps_dd = ctx.enter_context(tc.psum_pool(name="ps_dd", bufs=DD_BANKS))

        xraw = const.tile([P, PACK, P], BF16)
        nc.sync.dma_start(out=xraw[:], in_=X.rearrange("(p j) d -> p j d", j=PACK))
        raws = []
        units = []
        first_unit = []
        c0 = 0
        for b, w in enumerate(CHUNKS):
            r = rawp.tile([P, PACK, w], BF16, name="raw%d" % b)
            nc.sync.dma_start(
                out=r[:], in_=H[:, c0:c0 + w].rearrange("(p j) w -> p j w", j=PACK)
            )
            raws.append(r)
            first_unit.append(len(units))
            for g in range(w // GROUP):
                for th in range(TH):
                    units.append((b, g, th, (c0 + g * GROUP) // GROUP))
            c0 += w
        n_units = len(units)
        n_chunks = len(CHUNKS)

        ident = const.tile([P, P], F32)
        make_identity(nc, ident[:])
        ones = const.tile([P, PITCH], BF16)
        nc.vector.memset(ones[:], 1.0)
        warm = const.tile([P, 2], F32)
        nc.vector.memset(warm[:], 0.0)
        warm2 = const.tile([P, 2], F32)
        nc.scalar.activation(out=warm2[:], in_=warm[:], func=ACT.Copy)
        sel = const.tile([P, T, P], F32)
        nc.vector.memset(sel[:], 0.0)
        lane = const.tile([P, T], F32)
        nc.vector.tensor_reduce(
            out=lane[:], in_=ident[:].rearrange("p (g t) -> p t g", t=T),
            axis=mybir.AxisListType.X, op=ALU.add,
        )
        blk = const.tile([P, G], F32)
        nc.vector.tensor_reduce(
            out=blk[:], in_=ident[:].rearrange("p (g t) -> p g t", t=T),
            axis=mybir.AxisListType.X, op=ALU.add,
        )
        for c in range(T):
            nc.vector.tensor_copy(out=sel[:, c, c * G:(c + 1) * G], in_=blk[:])

        xg = const.tile([P, P, PACK], BF16, align_bytes=64)
        nc.vector.tensor_copy(out=xg[:], in_=xraw[:].rearrange("p j d -> p d j"))
        xcodes = const.tile([P, P], U32, align_bytes=64)
        xscales = const.tile([P, P], U8, align_bytes=64)

        dds = {}
        degs = {}
        invs = {}
        grouped = {}
        quantised = {}
        banks = {}
        otiles = {}

        def degree_sums(b):
            nt = CHUNKS[b] // P
            dd = ps_dd.tile([P, 512], F32, tag="dd")
            for c in range(nt):
                for j in range(PACK):
                    nc.tensor.matmul(
                        out=dd[:, c * PITCH:c * PITCH + ONES],
                        lhsT=raws[b][:, j, c * P:(c + 1) * P],
                        rhs=ones[:, 0:ONES], start=(j == 0), stop=(j == PACK - 1),
                    )
            dds[b] = dd

        def degree_spread(b):
            nt = CHUNKS[b] // P
            ng = CHUNKS[b] // GROUP
            dexp = small.tile([P, T, ng * T], F32, tag="dexp")
            nc.vector.tensor_tensor(
                out=dexp[:].rearrange("p c (g t) -> p c g t", t=T),
                in0=dds[b][:, 0:nt * PITCH].rearrange("p (g c n) -> p c g n", c=T, n=PITCH)
                [:, :, :, 0:1].to_broadcast([P, T, ng, T]),
                in1=lane[:].unsqueeze(1).unsqueeze(1).to_broadcast([P, T, ng, T]),
                op=ALU.mult,
            )
            for c in range(T):
                nc.tensor.matmul(
                    out=dds[b][:, D2_COL:D2_COL + ng * T], lhsT=sel[:, c, :], rhs=dexp[:, c, :],
                    start=(c == 0), stop=(c == T - 1),
                )

        def degree_copy(b):
            ng = CHUNKS[b] // GROUP
            deg = small.tile([P, ng * T], F32, tag="deg")
            nc.scalar.copy(out=deg[:], in_=dds[b][:, D2_COL:D2_COL + ng * T])
            degs[b] = deg

        def degree_invert(b):
            ng = CHUNKS[b] // GROUP
            deg = degs[b]
            safe = small.tile([P, ng * T], F32, tag="safe")
            nc.vector.scalar_tensor_tensor(
                out=safe[:], in0=deg[:], scalar=0.0, in1=deg[:],
                op0=ALU.is_equal, op1=ALU.add,
            )
            rec = small.tile([P, ng * T], F32, tag="rec")
            nc.vector.reciprocal(out=rec[:], in_=safe[:])
            inv = const.tile([P, ng * T], F32, name="inv%d" % b)
            nc.vector.scalar_tensor_tensor(
                out=inv[:], in0=deg[:], scalar=0.0, in1=rec[:],
                op0=ALU.not_equal, op1=ALU.mult,
            )
            invs[b] = inv

        def regroup(u, on_scalar):
            b, g, th, gg = units[u]
            if u % 2 == 0 and on_scalar:
                grouped[u // 2] = grp.tile(
                    [P, 2 * PACK * UNIT], BF16, align_bytes=64, tag="grouped", name="grouped"
                )
            half = (u % 2) * PACK * UNIT
            gt = grouped[u // 2][:, half:half + PACK * UNIT]
            block = raws[b][:, :, g * GROUP:(g + 1) * GROUP]
            src = block.rearrange("p j (q h i) -> p h q j i", h=TH, i=4)[:, th]
            dst = gt.rearrange("p (i q j) -> p q j i", i=4, j=PACK)
            if on_scalar:
                nc.scalar.copy(out=dst[:, QV:P], in_=src[:, QV:P])
            else:
                nc.vector.tensor_copy(out=dst[:, 0:QV], in_=src[:, 0:QV])

        def quantise(pair):
            codes = cod.tile([P, 2 * UNIT], U32, align_bytes=64, tag="codes")
            scales = cod.tile([P, 2 * UNIT], U8, align_bytes=64, tag="scales")
            nc.vector.quantize_mx(
                out=codes[:].bitcast(FP8X4), scales=scales[:], in_=grouped[pair][:]
            )
            quantised[pair] = (codes, scales)

        def multiply(u):
            codes, scales = quantised[u // 2]
            acc = ps_mx.tile([P, 512], F32, tag="acc")
            if u < n_units - 2:
                cols = slice((u % 2) * UNIT, (u % 2 + 1) * UNIT)
                nc.tensor.matmul_mx(
                    out=acc[:],
                    lhsT=xcodes[:].bitcast(FP8X4), lhsT_scale=xscales[:],
                    rhs=codes[:, cols].bitcast(FP8X4), rhs_scale=scales[:, cols],
                    start=True, stop=True,
                )
            for i in range(4):
                cols = slice((u % 2) * UNIT + i * P, (u % 2) * UNIT + (i + 1) * P)
                nc.tensor.matmul_mx(
                    out=acc[:, i * P:(i + 1) * P],
                    lhsT=codes[:, cols].bitcast(FP8X4), lhsT_scale=scales[:, cols],
                    rhs=xcodes[:].bitcast(FP8X4), rhs_scale=xscales[:],
                    start=True, stop=True,
                )
            banks[u] = acc

        def evacuate(u):
            b, g, th, gg = units[u]
            s = gg // STORE_GROUPS
            if s not in otiles:
                otiles[s] = outp.tile([P, STORE_GROUPS * T * P], F32, tag="o", name="o%d" % s)
            o = otiles[s]
            base = ((gg % STORE_GROUPS) * T + th * 4) * P
            if u >= n_units - 2:
                nc.vector.tensor_tensor(
                    out=o[:, base:base + UNIT].rearrange("p (t d) -> p t d", t=T),
                    in0=banks[u][:].rearrange("p (t d) -> p t d", t=T),
                    in1=invs[b][:, g * T:(g + 1) * T].unsqueeze(2).to_broadcast([P, T, P]),
                    op=ALU.mult,
                )
            else:
                for i in range(4):
                    k = g * T + th * 4 + i
                    nc.scalar.activation(
                        out=o[:, base + i * P:base + (i + 1) * P],
                        in_=banks[u][:, i * P:(i + 1) * P],
                        func=ACT.Copy, scale=invs[b][:, k:k + 1],
                    )
            if u >= n_units - 2:
                nc.sync.dma_start(
                    out=out[u * UNIT:(u + 1) * UNIT, :].rearrange("(q t) d -> q (t d)", t=T),
                    in_=o[:, base:base + UNIT],
                )
            elif gg % STORE_GROUPS == STORE_GROUPS - 1 and th == TH - 1:
                e0 = s * STORE_GROUPS * GROUP
                nc.sync.dma_start(
                    out=out[e0:e0 + STORE_GROUPS * GROUP, :]
                    .rearrange("(s q t) d -> q s (t d)", q=P, t=T),
                    in_=o[:].rearrange("q (s x) -> q s x", s=STORE_GROUPS),
                )

        for step in range(-2, n_units + EV_LAG):
            for b in range(n_chunks):
                if first_unit[b] + 2 == step:
                    degree_copy(b)
            if 0 <= step + 2 < n_units:
                regroup(step + 2, True)
            if 0 <= step + 1 < n_units:
                regroup(step + 1, False)
            if step == -1:
                nc.vector.quantize_mx(
                    out=xcodes[:].bitcast(FP8X4), scales=xscales[:],
                    in_=xg[:].rearrange("p d j -> p (d j)"),
                )
            if 0 <= step < n_units and step % 2 == 1:
                quantise(step // 2)
                multiply(step - 1)
                multiply(step)
            for b in range(n_chunks):
                if first_unit[b] == step:
                    degree_spread(b)
                if first_unit[b] + 2 == step:
                    degree_invert(b)
                if first_unit[b] - 2 == step:
                    degree_sums(b)
            if 0 <= step - EV_LAG < n_units:
                evacuate(step - EV_LAG)
